import numpy as np
import ml_dtypes


def mxq(x, axis, fmt="e4m3"):
    dtype, down = {"e4m3": (ml_dtypes.float8_e4m3fn, 7), "e5m2": (ml_dtypes.float8_e5m2, 14)}[fmt]
    v = np.moveaxis(np.asarray(x, np.float32).astype(ml_dtypes.bfloat16).astype(np.float64), axis, -1)
    blocks = v.reshape(v.shape[:-1] + (-1, 32))
    amax = np.abs(blocks).max(-1, keepdims=True)
    byte = np.maximum(np.where(amax > 0, np.frexp(amax)[1] - 1 + 127, 0) - down, 1)
    scale = np.exp2(byte - 127.0)
    codes = (blocks / scale).astype(np.float32).astype(dtype).astype(np.float64)
    return np.moveaxis((codes * scale).reshape(v.shape), -1, axis)


WIDE = False


def mx_kscale(k):
    if not WIDE:
        return np.ones(k)
    levels = np.array([10, -10, 5, -5, 0])
    a = np.random.permutation(np.resize(levels, k // 512 * 4)).reshape(k // 512, 4)
    idx = np.arange(k)
    return np.exp2(a[idx // 512, idx % 128 // 32])


BF16 = ml_dtypes.bfloat16


def bf(x):
    return np.asarray(x, np.float32).astype(BF16)


def f64(x):
    return np.asarray(x).astype(np.float64)


E2M1 = np.array([0.0, 0.5, 1.0, 1.5, 2.0, 3.0, 4.0, 6.0, -0.0, -0.5, -1.0, -1.5, -2.0, -3.0, -4.0, -6.0])


def pack_weight(w, fmt):
    k, n = w.shape
    w = f64(bf(w)).reshape(k // 32, 32, n)
    amax = np.abs(w).max(1)
    if fmt == "e4m3":
        byte = np.frexp(amax)[1] - 1 + 127 - 7
    else:
        mant, ex = np.frexp(amax / 6.0)
        byte = np.where(mant > 0.5, ex, ex - 1) + 127
    byte = np.clip(np.where(amax > 0, byte, 1), 1, 254)
    scaled = (w * np.exp2(127.0 - byte)[:, None, :]).reshape(k, n).astype(np.float32)
    by_word = np.ascontiguousarray(scaled.reshape(k // 512, 128, 4, n).transpose(0, 1, 3, 2))
    if fmt == "e4m3":
        words = by_word.astype(ml_dtypes.float8_e4m3fn).view(np.uint8)
    else:
        c = by_word.astype(ml_dtypes.float4_e2m1fn).view(np.uint8) & 0xF
        words = c[..., 0::2] | (c[..., 1::2] << 4)
    return np.ascontiguousarray(words), np.ascontiguousarray(byte.astype(np.uint8).reshape(k // 512, 16, n))


def unpack_weight(words, scales, fmt):
    g, p, n, _ = words.shape
    if fmt == "e4m3":
        vals = np.ascontiguousarray(words).view(ml_dtypes.float8_e4m3fn).astype(np.float64)
    else:
        nib = np.empty((g, p, n, 4), np.uint8)
        nib[..., 0::2] = words & 0xF
        nib[..., 1::2] = words >> 4
        vals = E2M1[nib]
    vals = vals * np.repeat(np.exp2(scales.astype(np.float64) - 127.0), 8, axis=1)[..., None]
    return vals.transpose(0, 1, 3, 2).reshape(g * 512, n)

def pack4(w):
    words, scales = pack_weight(w, "e2m1")
    return words.reshape(words.shape[0], 128, -1), scales


def unpack4(words, scales):
    return unpack_weight(words.reshape(words.shape[0], 128, -1, 2), scales, "e2m1")


B, S, C, E, H = 4, 64, 16384, 256, 16
ROPE_BASE = 10000.0
NORM_EPS = 1e-12
INV_FREQ = ROPE_BASE ** (-(np.arange(0, E, 2) / E))
THETA = S * np.repeat(INV_FREQ, 2)
SIN, COS = np.sin(THETA), np.cos(THETA)


def rotate(t):
    t1 = t[..., :-1:2]
    t2 = t[..., 1::2]
    t_rot = np.concatenate((-t2, t1), axis=-1)
    return t * COS + t_rot * SIN


def l2_normalize(t):
    n = np.sqrt((t * t).sum(-1, keepdims=True))
    return t / np.maximum(n, NORM_EPS)


def setup_inputs():
    s = mx_kscale(C)
    x = bf(np.random.standard_normal((B, S, C)) * s)
    w = np.random.standard_normal((3 * E, C)) / np.sqrt(C) / s
    words, scales = pack4(np.ascontiguousarray(w.T))
    bqkv = bf(np.random.standard_normal(3 * E) * 0.3)
    return {"x": x, "Wqkv_words": words, "Wqkv_scales": scales, "bqkv": bqkv}


def reference(x, Wqkv_words, Wqkv_scales, bqkv):
    xq = mxq(f64(x), 2, "e4m3")
    wq = unpack4(Wqkv_words, Wqkv_scales).T
    b = f64(bqkv)
    q = (xq @ wq[:E].T) + b[:E]
    k = (xq @ wq[E:2 * E].T) + b[E:2 * E]
    v = (xq @ wq[2 * E:].T) + b[2 * E:]
    return l2_normalize(rotate(q)), l2_normalize(rotate(k)), v

@@ -1,0 +1,383 @@
+import math
+from contextlib import ExitStack
+
+import concourse.mybir as mybir
+from concourse.masks import make_identity
+
+F32 = mybir.dt.float32
+BF16 = mybir.dt.bfloat16
+I32 = mybir.dt.int32
+U32 = mybir.dt.uint32
+U8 = mybir.dt.uint8
+FP8X4 = mybir.dt.float8_e4m3fn_x4
+FP4X4 = mybir.dt.float4_e2m1fn_x4
+ALU = mybir.AluOpType
+ACT = mybir.ActivationFunctionType
+
+P = 128
+TOKENS = 256
+TOKEN_TILES = TOKENS // P
+K = 16384
+K_PASS = 4 * P
+PASSES = K // K_PASS
+ROUND = 4
+ROUNDS = PASSES // ROUND
+PAIR = 2
+E = 256
+N_QK = 2 * E
+N_V = 128
+V_HALVES = E // N_V
+N_ALL = 3 * E
+SCALE_ROWS = K_PASS // 32
+
+FLOPS = 2 * TOKENS * K * N_ALL
+
+SEQ = 64.0
+ROPE_BASE = 10000.0
+ANGLES = E // 2
+ANGLE_RATIO = ROPE_BASE ** (-1.0 / ANGLES)
+ANGLE_DOUBLINGS = 7
+assert 2**ANGLE_DOUBLINGS == ANGLES
+NORM_EPS = 1e-12
+ROUND_MAGIC = 12582912.0
+TWO_PI_HIGH = 6.28125
+TWO_PI_LOW = 2.0 * math.pi - TWO_PI_HIGH
+
+
+def tile_multiheadattention_pa_k_kernel(
+    tc, x, Wqkv_words, Wqkv_scales, bqkv, out_0, out_1, out_2
+):
+    nc = tc.nc
+    x_rows = x.flatten_outer_dims()
+    qk_rows = [out_0.flatten_outer_dims(), out_1.flatten_outer_dims()]
+    v_rows = out_2.flatten_outer_dims()
+
+    with ExitStack() as stack:
+        keep = stack.enter_context(tc.tile_pool(name="keep", bufs=1))
+        stream = stack.enter_context(tc.tile_pool(name="stream", bufs=2))
+        psum = stack.enter_context(tc.psum_pool(name="psum", bufs=1))
+        stack.enter_context(tc.manual_schedule())
+
+        x_raw = [
+            keep.tile([P, TOKEN_TILES, ROUND * K_PASS], BF16, name="x_raw%d" % r)
+            for r in range(ROUNDS)
+        ]
+        w_words = [
+            keep.tile([P, ROUND, 2 * N_ALL], U8, name="w_words%d" % r, align_bytes=64)
+            for r in range(ROUNDS)
+        ]
+        w_scales = [
+            keep.tile([P, ROUND, N_ALL], U8, name="w_scales%d" % r, align_bytes=64)
+            for r in range(ROUNDS)
+        ]
+        identity = keep.tile([P, P], F32, name="identity")
+        ones = keep.tile([P, P], BF16, name="ones")
+        bias_row = keep.tile([P, N_ALL], BF16, name="bias_row")
+        bias_qk = keep.tile([P, N_QK], F32, name="bias_qk")
+        v_sum = keep.tile([P, TOKEN_TILES, E], F32, name="v_sum")
+        cos_full = keep.tile([P, N_QK], F32, name="cos_full")
+        sin_full = keep.tile([P, N_QK], F32, name="sin_full")
+        acc_qk = [psum.tile([P, N_QK], F32, name="acc_qk%d" % tt) for tt in range(TOKEN_TILES)]
+
+        make_identity(nc, identity[:])
+
+        nc.vector.memset(bias_row[:], 0.0)
+        nc.scalar.dma_start(out=bias_row[0:1, :], in_=bqkv.rearrange("(o n) -> o n", o=1))
+        nc.vector.memset(ones[:], 1.0)
+
+        for r in range(ROUNDS):
+            nc.vector.memset(w_scales[r][:].bitcast(I32), 0)
+
+        def load_x(r):
+            columns = slice(r * ROUND * K_PASS, (r + 1) * ROUND * K_PASS)
+            for tt in range(TOKEN_TILES):
+                nc.sync.dma_start(
+                    out=x_raw[r][:, tt, :], in_=x_rows[tt * P : (tt + 1) * P, columns]
+                )
+
+        def load_w_words(r):
+            nc.sync.dma_start(
+                out=w_words[r][:].bitcast(I32),
+                in_=Wqkv_words[r * ROUND : (r + 1) * ROUND]
+                .rearrange("g p b -> p g b")
+                .bitcast(I32),
+            )
+
+        def load_w_scales(r):
+            for first_q in range(SCALE_ROWS // 2):
+                first_partition = 32 * (first_q // 4) + first_q % 4
+                nc.sync.dma_start(
+                    out=w_scales[r][first_partition:P:64, :, :].bitcast(I32),
+                    in_=Wqkv_scales[r * ROUND : (r + 1) * ROUND, first_q : SCALE_ROWS : 8, :]
+                    .rearrange("g q n -> q g n")
+                    .bitcast(I32),
+                )
+
+        load_x(0)
+        load_x(1)
+        for r in range(ROUNDS):
+            if r % 2 == 0:
+                load_w_scales(r)
+                load_w_scales(r + 1)
+            load_w_words(r)
+            if r + 2 < ROUNDS:
+                load_x(r + 2)
+
+        bias_qk_ps = psum.tile([P, N_QK], F32, name="bias_qk_ps", tag="transposed", bufs=4)
+        nc.tensor.matmul(
+            out=bias_qk_ps[:], lhsT=ones[:], rhs=bias_row[:, 0:N_QK], start=True, stop=True
+        )
+        bias_v_ps = psum.tile([P, E], F32, name="bias_v_ps", tag="transposed", bufs=4)
+        nc.tensor.matmul(
+            out=bias_v_ps[:], lhsT=ones[:], rhs=bias_row[:, N_QK:N_ALL], start=True, stop=True
+        )
+
+        angle = keep.tile([P, ANGLES], F32, name="angle")
+        nc.vector.memset(angle[:, 0:1], SEQ)
+        for doubling in range(ANGLE_DOUBLINGS):
+            span = 2**doubling
+            nc.vector.tensor_scalar_mul(
+                out=angle[:, span : 2 * span], in0=angle[:, 0:span], scalar1=ANGLE_RATIO**span
+            )
+        turns = keep.tile([P, ANGLES], F32, name="turns")
+        nc.vector.tensor_scalar(
+            out=turns[:],
+            in0=angle[:],
+            scalar1=1.0 / (2.0 * math.pi),
+            scalar2=ROUND_MAGIC,
+            op0=ALU.mult,
+            op1=ALU.add,
+        )
+        nc.vector.tensor_scalar_sub(out=turns[:], in0=turns[:], scalar1=ROUND_MAGIC)
+        reduced = keep.tile([P, ANGLES], F32, name="reduced")
+        nc.vector.scalar_tensor_tensor(
+            out=reduced[:],
+            in0=turns[:],
+            scalar=-TWO_PI_HIGH,
+            in1=angle[:],
+            op0=ALU.mult,
+            op1=ALU.add,
+        )
+        nc.vector.scalar_tensor_tensor(
+            out=reduced[:],
+            in0=turns[:],
+            scalar=-TWO_PI_LOW,
+            in1=reduced[:],
+            op0=ALU.mult,
+            op1=ALU.add,
+        )
+        quarter_minus_abs = keep.tile([P, ANGLES], F32, name="quarter_minus_abs")
+        nc.vector.scalar_tensor_tensor(
+            out=quarter_minus_abs[:],
+            in0=reduced[:],
+            scalar=-1.0,
+            in1=reduced[:],
+            op0=ALU.mult,
+            op1=ALU.max,
+        )
+        nc.vector.tensor_scalar(
+            out=quarter_minus_abs[:],
+            in0=quarter_minus_abs[:],
+            scalar1=-1.0,
+            scalar2=math.pi / 2.0,
+            op0=ALU.mult,
+            op1=ALU.add,
+        )
+        nc.scalar.activation(
+            out=cos_full[:].rearrange("p (h j e) -> p h j e", h=2, e=2),
+            in_=quarter_minus_abs[:].unsqueeze(1).unsqueeze(3).to_broadcast([P, 2, ANGLES, 2]),
+            func=ACT.Sin,
+        )
+        sin_halves = sin_full[:].rearrange("p (h f j e) -> p h f j e", h=2, f=2, e=2)
+        for f in range(2):
+            nc.scalar.activation(
+                out=sin_halves[:, :, f, :, :],
+                in_=reduced[:, f * (ANGLES // 2) : (f + 1) * (ANGLES // 2)]
+                .unsqueeze(1)
+                .unsqueeze(3)
+                .to_broadcast([P, 2, ANGLES // 2, 2]),
+                func=ACT.Sin,
+                scale=(-1.0 if f == 0 else 1.0),
+            )
+        sqrt_warm = keep.tile([P, 1], F32, name="sqrt_warm")
+        nc.scalar.sqrt(out=sqrt_warm[:], in_=angle[:, 0:1])
+
+        nc.scalar.copy(out=bias_qk[:], in_=bias_qk_ps[:])
+        for tt in range(TOKEN_TILES):
+            nc.scalar.copy(out=v_sum[:, tt, :], in_=bias_v_ps[:])
+
+        sorted_x = {}
+        grouped = {}
+        x_words = {}
+        x_scales = {}
+        v_part = {}
+
+        def sort_words(r):
+            sorted_x[r] = stream.tile([P, TOKEN_TILES, ROUND, 2, P], F32, name="sorted_x")
+            for tt in range(TOKEN_TILES):
+                nc.vector.tensor_copy(
+                    out=sorted_x[r][:, tt, :, :, :],
+                    in_=x_raw[r][:, tt, :]
+                    .bitcast(F32)
+                    .rearrange("p (g w u) -> p g u w", g=ROUND, u=2),
+                )
+
+        def transpose_and_regroup(r):
+            grouped[r] = stream.tile(
+                [P, TOKEN_TILES, ROUND, 4 * P], BF16, name="grouped", align_bytes=64
+            )
+            banks = {}
+            for tt in range(TOKEN_TILES):
+                for pair in range(ROUND // PAIR):
+                    bank = psum.tile([P, PAIR, 2, P], F32, name="bank", tag="transposed", bufs=4)
+                    banks[(tt, pair)] = bank
+                    for a in range(PAIR):
+                        for u in range(2):
+                            nc.tensor.transpose(
+                                out=bank[:, a, u, :],
+                                in_=sorted_x[r][:, tt, pair * PAIR + a, u, :],
+                                identity=identity[:],
+                            )
+            for tt in range(TOKEN_TILES):
+                for pair in range(ROUND // PAIR):
+                    nc.scalar.copy(
+                        out=grouped[r][:, tt, pair * PAIR : (pair + 1) * PAIR, :]
+                        .bitcast(F32)
+                        .rearrange("p a (t u) -> p a t u", u=2),
+                        in_=banks[(tt, pair)][:].rearrange("p a u t -> p a t u"),
+                    )
+
+        def quantise(r):
+            x_words[r] = stream.tile(
+                [P, TOKEN_TILES, ROUND, P], U32, name="x_words", align_bytes=64
+            )
+            x_scales[r] = stream.tile(
+                [P, TOKEN_TILES, ROUND, P], U8, name="x_scales", align_bytes=64
+            )
+            for tt in range(TOKEN_TILES):
+                nc.vector.quantize_mx(
+                    out=x_words[r][:, tt, :, :].rearrange("p g t -> p (g t)").bitcast(FP8X4),
+                    scales=x_scales[r][:, tt, :, :].rearrange("p g t -> p (g t)"),
+                    in_=grouped[r][:, tt, :, :].rearrange("p g c -> p (g c)"),
+                )
+
+        def mx_pass(out, r, tt, g, first_column, columns, start, stop):
+            nc.tensor.matmul_mx(
+                out=out,
+                lhsT=x_words[r][:, tt, g, :].bitcast(FP8X4),
+                lhsT_scale=x_scales[r][:, tt, g, :],
+                rhs=w_words[r][:, g, 2 * first_column : 2 * (first_column + columns)].bitcast(
+                    FP4X4
+                ),
+                rhs_scale=w_scales[r][:, g, first_column : first_column + columns],
+                start=start,
+                stop=stop,
+            )
+
+        def multiply(r):
+            for tt in range(TOKEN_TILES):
+                for g in range(ROUND):
+                    mx_pass(
+                        acc_qk[tt][:],
+                        r,
+                        tt,
+                        g,
+                        0,
+                        N_QK,
+                        start=(r == 0 and g == 0),
+                        stop=(r == ROUNDS - 1 and g == ROUND - 1),
+                    )
+            v_part[r] = psum.tile([P, TOKEN_TILES, V_HALVES, N_V], F32, name="v_part", bufs=2)
+            for tt in range(TOKEN_TILES):
+                for half in range(V_HALVES):
+                    for g in range(ROUND):
+                        mx_pass(
+                            v_part[r][:, tt, half, :],
+                            r,
+                            tt,
+                            g,
+                            N_QK + half * N_V,
+                            N_V,
+                            start=(g == 0),
+                            stop=(g == ROUND - 1),
+                        )
+
+        def add_v(r):
+            nc.vector.tensor_tensor(
+                out=v_sum[:].rearrange("p t e -> p (t e)"),
+                in0=v_part[r][:].rearrange("p t h n -> p (t h n)"),
+                in1=v_sum[:].rearrange("p t e -> p (t e)"),
+                op=ALU.add,
+            )
+
+        sort_words(0)
+        for r in range(ROUNDS + 1):
+            if r >= 1:
+                quantise(r - 1)
+            if r + 1 < ROUNDS:
+                sort_words(r + 1)
+            if r >= 2:
+                add_v(r - 2)
+            if r < ROUNDS:
+                transpose_and_regroup(r)
+            if r >= 1:
+                multiply(r - 1)
+
+        mixed = {}
+        norm = {}
+
+        def mix(tt):
+            t = stream.tile([P, N_QK], F32, name="t")
+            nc.vector.tensor_tensor(out=t[:], in0=acc_qk[tt][:], in1=bias_qk[:], op=ALU.add)
+            t_cos = stream.tile([P, N_QK], F32, name="t_cos")
+            nc.vector.tensor_tensor(out=t_cos[:], in0=t[:], in1=cos_full[:], op=ALU.mult)
+            rot_sin = stream.tile([P, N_QK], F32, name="rot_sin")
+            t_pairs = t[:].rearrange("p (h i e) -> p h i e", h=2, e=2)
+            rot_halves = rot_sin[:].rearrange("p (h f i) -> p h f i", h=2, f=2)
+            sin_by_half = sin_full[:].rearrange("p (h f i) -> p h f i", h=2, f=2)
+            for f in range(2):
+                nc.vector.tensor_tensor(
+                    out=rot_halves[:, :, f, :],
+                    in0=t_pairs[:, :, :, 1 - f],
+                    in1=sin_by_half[:, :, f, :],
+                    op=ALU.mult,
+                )
+            mixed[tt] = stream.tile([P, 2, E], F32, name="mixed")
+            nc.vector.tensor_tensor(
+                out=mixed[tt][:].rearrange("p h e -> p (h e)"),
+                in0=t_cos[:],
+                in1=rot_sin[:],
+                op=ALU.add,
+            )
+            squares = stream.tile([P, 2, E], F32, name="squares")
+            square_sum = stream.tile([P, 2], F32, name="square_sum")
+            for h in range(2):
+                nc.scalar.activation(
+                    out=squares[:, h, :],
+                    in_=mixed[tt][:, h, :],
+                    func=ACT.Square,
+                    accum_out=square_sum[:, h : h + 1],
+                )
+            norm[tt] = stream.tile([P, 2], F32, name="norm")
+            nc.scalar.sqrt(out=norm[tt][:], in_=square_sum[:])
+
+        def normalise_and_store(tt):
+            inverse = stream.tile([P, 2], F32, name="inverse")
+            nc.vector.tensor_scalar_max(out=inverse[:], in0=norm[tt][:], scalar1=NORM_EPS)
+            nc.vector.reciprocal(out=inverse[:], in_=inverse[:])
+            unit = stream.tile([P, 2, E], F32, name="unit")
+            nc.vector.tensor_scalar_mul(
+                out=unit[:, 0, :], in0=mixed[tt][:, 0, :], scalar1=inverse[:, 0:1]
+            )
+            nc.scalar.activation(
+                out=unit[:, 1, :], in_=mixed[tt][:, 1, :], func=ACT.Copy, scale=inverse[:, 1:2]
+            )
+            for h in range(2):
+                nc.sync.dma_start(out=qk_rows[h][tt * P : (tt + 1) * P, :], in_=unit[:, h, :])
+
+        mix(0)
+        mix(1)
+        normalise_and_store(0)
+        add_v(ROUNDS - 1)
+        nc.sync.dma_start(out=v_rows.rearrange("(t p) e -> p t e", p=P), in_=v_sum[:])
+        normalise_and_store(1)

@@ -29,6 +29,7 @@ N_V = 128
 V_HALVES = E // N_V
 N_ALL = 3 * E
 SCALE_ROWS = K_PASS // 32
+FIRST_SCALES = 2 * ROUND
 
 FLOPS = 2 * TOKENS * K * N_ALL
 
@@ -66,10 +67,7 @@ def tile_multiheadattention_pa_k_kernel(
             keep.tile([P, ROUND, 2 * N_ALL], U8, name="w_words%d" % r, align_bytes=64)
             for r in range(ROUNDS)
         ]
-        w_scales = [
-            keep.tile([P, ROUND, N_ALL], U8, name="w_scales%d" % r, align_bytes=64)
-            for r in range(ROUNDS)
-        ]
+        w_scales = keep.tile([P, PASSES, N_ALL], U8, name="w_scales", align_bytes=64)
         identity = keep.tile([P, P], F32, name="identity")
         ones = keep.tile([P, P], BF16, name="ones")
         bias_row = keep.tile([P, N_ALL], BF16, name="bias_row")
@@ -85,8 +83,15 @@ def tile_multiheadattention_pa_k_kernel(
         nc.scalar.dma_start(out=bias_row[0:1, :], in_=bqkv.rearrange("(o n) -> o n", o=1))
         nc.vector.memset(ones[:], 1.0)
 
-        for r in range(ROUNDS):
-            nc.vector.memset(w_scales[r][:].bitcast(I32), 0)
+        for batch in (slice(0, FIRST_SCALES), slice(FIRST_SCALES, PASSES)):
+            nc.vector.memset(w_scales[:, batch, :].bitcast(I32), 0)
+            for i in range(4):
+                nc.gpsimd.dma_start(
+                    out=w_scales[i:P:32, batch, :].bitcast(F32),
+                    in_=Wqkv_scales[batch, i:SCALE_ROWS:4, :]
+                    .rearrange("g q n -> q g n")
+                    .bitcast(F32),
+                )
 
         def load_x(r):
             columns = slice(r * ROUND * K_PASS, (r + 1) * ROUND * K_PASS)
@@ -103,22 +108,9 @@ def tile_multiheadattention_pa_k_kernel(
                 .bitcast(I32),
             )
 
-        def load_w_scales(r):
-            for first_q in range(SCALE_ROWS // 2):
-                first_partition = 32 * (first_q // 4) + first_q % 4
-                nc.sync.dma_start(
-                    out=w_scales[r][first_partition:P:64, :, :].bitcast(I32),
-                    in_=Wqkv_scales[r * ROUND : (r + 1) * ROUND, first_q : SCALE_ROWS : 8, :]
-                    .rearrange("g q n -> q g n")
-                    .bitcast(I32),
-                )
-
         load_x(0)
         load_x(1)
         for r in range(ROUNDS):
-            if r % 2 == 0:
-                load_w_scales(r)
-                load_w_scales(r + 1)
             load_w_words(r)
             if r + 2 < ROUNDS:
                 load_x(r + 2)
@@ -269,7 +261,7 @@ def tile_multiheadattention_pa_k_kernel(
                 rhs=w_words[r][:, g, 2 * first_column : 2 * (first_column + columns)].bitcast(
                     FP4X4
                 ),
-                rhs_scale=w_scales[r][:, g, first_column : first_column + columns],
+                rhs_scale=w_scales[:, r * ROUND + g, first_column : first_column + columns],
                 start=start,
                 stop=stop,
             )

@@ -29,7 +29,11 @@ N_V = 128
 V_HALVES = E // N_V
 N_ALL = 3 * E
 SCALE_ROWS = K_PASS // 32
-FIRST_SCALES = 2 * ROUND
+BATCH_ROUNDS = 2
+SCALE_BATCH = BATCH_ROUNDS * ROUND
+BATCHES = PASSES // SCALE_BATCH
+V_LAST = 4
+V_STREAMED = ROUNDS - V_LAST
 
 FLOPS = 2 * TOKENS * K * N_ALL
 
@@ -67,7 +71,10 @@ def tile_multiheadattention_pa_k_kernel(
             keep.tile([P, ROUND, 2 * N_ALL], U8, name="w_words%d" % r, align_bytes=64)
             for r in range(ROUNDS)
         ]
-        w_scales = keep.tile([P, PASSES, N_ALL], U8, name="w_scales", align_bytes=64)
+        w_scales = [
+            keep.tile([P, SCALE_BATCH, N_ALL], U8, name="w_scales%d" % batch, align_bytes=64)
+            for batch in range(BATCHES)
+        ]
         identity = keep.tile([P, P], F32, name="identity")
         ones = keep.tile([P, P], BF16, name="ones")
         bias_row = keep.tile([P, N_ALL], BF16, name="bias_row")
@@ -83,15 +90,18 @@ def tile_multiheadattention_pa_k_kernel(
         nc.scalar.dma_start(out=bias_row[0:1, :], in_=bqkv.rearrange("(o n) -> o n", o=1))
         nc.vector.memset(ones[:], 1.0)
 
-        for batch in (slice(0, FIRST_SCALES), slice(FIRST_SCALES, PASSES)):
-            nc.vector.memset(w_scales[:, batch, :].bitcast(I32), 0)
-            for i in range(4):
-                nc.gpsimd.dma_start(
-                    out=w_scales[i:P:32, batch, :].bitcast(F32),
-                    in_=Wqkv_scales[batch, i:SCALE_ROWS:4, :]
-                    .rearrange("g q n -> q g n")
-                    .bitcast(F32),
-                )
+        def spread_bias():
+            bias_qk_ps = psum.tile([P, N_QK], F32, name="bias_qk_ps", tag="v_part", bufs=2)
+            nc.tensor.matmul(
+                out=bias_qk_ps[:], lhsT=ones[:], rhs=bias_row[:, 0:N_QK], start=True, stop=True
+            )
+            bias_v_ps = psum.tile([P, E], F32, name="bias_v_ps", tag="v_part", bufs=2)
+            nc.tensor.matmul(
+                out=bias_v_ps[:], lhsT=ones[:], rhs=bias_row[:, N_QK:N_ALL], start=True, stop=True
+            )
+            nc.vector.tensor_copy(out=bias_qk[:], in_=bias_qk_ps[:])
+            for tt in range(TOKEN_TILES):
+                nc.vector.tensor_copy(out=v_sum[:, tt, :], in_=bias_v_ps[:])
 
         def load_x(r):
             columns = slice(r * ROUND * K_PASS, (r + 1) * ROUND * K_PASS)
@@ -108,21 +118,27 @@ def tile_multiheadattention_pa_k_kernel(
                 .bitcast(I32),
             )
 
+        def load_w_scales(batch):
+            nc.vector.memset(w_scales[batch][:].bitcast(I32), 0)
+            passes = slice(batch * SCALE_BATCH, (batch + 1) * SCALE_BATCH)
+            for i in range(4):
+                nc.sync.dma_start(
+                    out=w_scales[batch][i:P:32, :, :].bitcast(I32),
+                    in_=Wqkv_scales[passes, i:SCALE_ROWS:4, :]
+                    .rearrange("g q n -> q g n")
+                    .bitcast(I32),
+                )
+
+        def load_batch(batch):
+            load_w_scales(batch)
+            for r in range(batch * BATCH_ROUNDS, (batch + 1) * BATCH_ROUNDS):
+                load_w_words(r)
+                if r + 2 < ROUNDS:
+                    load_x(r + 2)
+
         load_x(0)
         load_x(1)
-        for r in range(ROUNDS):
-            load_w_words(r)
-            if r + 2 < ROUNDS:
-                load_x(r + 2)
-
-        bias_qk_ps = psum.tile([P, N_QK], F32, name="bias_qk_ps", tag="transposed", bufs=4)
-        nc.tensor.matmul(
-            out=bias_qk_ps[:], lhsT=ones[:], rhs=bias_row[:, 0:N_QK], start=True, stop=True
-        )
-        bias_v_ps = psum.tile([P, E], F32, name="bias_v_ps", tag="transposed", bufs=4)
-        nc.tensor.matmul(
-            out=bias_v_ps[:], lhsT=ones[:], rhs=bias_row[:, N_QK:N_ALL], start=True, stop=True
-        )
+        load_batch(0)
 
         angle = keep.tile([P, ANGLES], F32, name="angle")
         nc.vector.memset(angle[:, 0:1], SEQ)
@@ -191,13 +207,6 @@ def tile_multiheadattention_pa_k_kernel(
                 func=ACT.Sin,
                 scale=(-1.0 if f == 0 else 1.0),
             )
-        sqrt_warm = keep.tile([P, 1], F32, name="sqrt_warm")
-        nc.scalar.sqrt(out=sqrt_warm[:], in_=angle[:, 0:1])
-
-        nc.scalar.copy(out=bias_qk[:], in_=bias_qk_ps[:])
-        for tt in range(TOKEN_TILES):
-            nc.scalar.copy(out=v_sum[:, tt, :], in_=bias_v_ps[:])
-
         sorted_x = {}
         grouped = {}
         x_words = {}
@@ -241,10 +250,10 @@ def tile_multiheadattention_pa_k_kernel(
 
         def quantise(r):
             x_words[r] = stream.tile(
-                [P, TOKEN_TILES, ROUND, P], U32, name="x_words", align_bytes=64
+                [P, TOKEN_TILES, ROUND, P], U32, name="x_words", bufs=V_LAST, align_bytes=64
             )
             x_scales[r] = stream.tile(
-                [P, TOKEN_TILES, ROUND, P], U8, name="x_scales", align_bytes=64
+                [P, TOKEN_TILES, ROUND, P], U8, name="x_scales", bufs=V_LAST, align_bytes=64
             )
             for tt in range(TOKEN_TILES):
                 nc.vector.quantize_mx(
@@ -254,6 +263,7 @@ def tile_multiheadattention_pa_k_kernel(
                 )
 
         def mx_pass(out, r, tt, g, first_column, columns, start, stop):
+            batch, pass_in_batch = divmod(r * ROUND + g, SCALE_BATCH)
             nc.tensor.matmul_mx(
                 out=out,
                 lhsT=x_words[r][:, tt, g, :].bitcast(FP8X4),
@@ -261,12 +271,14 @@ def tile_multiheadattention_pa_k_kernel(
                 rhs=w_words[r][:, g, 2 * first_column : 2 * (first_column + columns)].bitcast(
                     FP4X4
                 ),
-                rhs_scale=w_scales[:, r * ROUND + g, first_column : first_column + columns],
+                rhs_scale=w_scales[batch][
+                    :, pass_in_batch, first_column : first_column + columns
+                ],
                 start=start,
                 stop=stop,
             )
 
-        def multiply(r):
+        def multiply_qk(r):
             for tt in range(TOKEN_TILES):
                 for g in range(ROUND):
                     mx_pass(
@@ -279,41 +291,54 @@ def tile_multiheadattention_pa_k_kernel(
                         start=(r == 0 and g == 0),
                         stop=(r == ROUNDS - 1 and g == ROUND - 1),
                     )
-            v_part[r] = psum.tile([P, TOKEN_TILES, V_HALVES, N_V], F32, name="v_part", bufs=2)
+
+        def multiply_v(first_round, rounds):
+            v_part[first_round] = psum.tile(
+                [P, TOKEN_TILES, V_HALVES, N_V], F32, name="v_part", bufs=2
+            )
             for tt in range(TOKEN_TILES):
                 for half in range(V_HALVES):
-                    for g in range(ROUND):
-                        mx_pass(
-                            v_part[r][:, tt, half, :],
-                            r,
-                            tt,
-                            g,
-                            N_QK + half * N_V,
-                            N_V,
-                            start=(g == 0),
-                            stop=(g == ROUND - 1),
-                        )
+                    for r in range(first_round, first_round + rounds):
+                        for g in range(ROUND):
+                            mx_pass(
+                                v_part[first_round][:, tt, half, :],
+                                r,
+                                tt,
+                                g,
+                                N_QK + half * N_V,
+                                N_V,
+                                start=(r == first_round and g == 0),
+                                stop=(r == first_round + rounds - 1 and g == ROUND - 1),
+                            )
 
-        def add_v(r):
+        def add_v(first_round):
             nc.vector.tensor_tensor(
                 out=v_sum[:].rearrange("p t e -> p (t e)"),
-                in0=v_part[r][:].rearrange("p t h n -> p (t h n)"),
+                in0=v_part[first_round][:].rearrange("p t h n -> p (t h n)"),
                 in1=v_sum[:].rearrange("p t e -> p (t e)"),
                 op=ALU.add,
             )
 
         sort_words(0)
-        for r in range(ROUNDS + 1):
-            if r >= 1:
-                quantise(r - 1)
+        transpose_and_regroup(0)
+        sqrt_warm = keep.tile([P, 1], F32, name="sqrt_warm")
+        nc.scalar.sqrt(out=sqrt_warm[:], in_=angle[:, 0:1])
+        sort_words(1)
+        spread_bias()
+        for r in range(1, ROUNDS + 1):
+            quantise(r - 1)
             if r + 1 < ROUNDS:
                 sort_words(r + 1)
-            if r >= 2:
+            if 0 <= r - 2 < V_STREAMED:
                 add_v(r - 2)
+            if r < BATCHES:
+                load_batch(r)
             if r < ROUNDS:
                 transpose_and_regroup(r)
-            if r >= 1:
-                multiply(r - 1)
+            multiply_qk(r - 1)
+            if r - 1 < V_STREAMED:
+                multiply_v(r - 1, 1)
+        multiply_v(V_STREAMED, V_LAST)
 
         mixed = {}
         norm = {}
@@ -370,6 +395,6 @@ def tile_multiheadattention_pa_k_kernel(
         mix(0)
         mix(1)
         normalise_and_store(0)
-        add_v(ROUNDS - 1)
+        add_v(V_STREAMED)
         nc.sync.dma_start(out=v_rows.rearrange("(t p) e -> p t e", p=P), in_=v_sum[:])
         normalise_and_store(1)

@@ -118,27 +118,26 @@ def tile_multiheadattention_pa_k_kernel(
                 .bitcast(I32),
             )
 
-        def load_w_scales(batch):
-            nc.vector.memset(w_scales[batch][:].bitcast(I32), 0)
+        def load_w_scales(batch, zeroing_engine, queue, word):
+            zeroing_engine.memset(w_scales[batch][:].bitcast(word), 0)
             passes = slice(batch * SCALE_BATCH, (batch + 1) * SCALE_BATCH)
             for i in range(4):
-                nc.sync.dma_start(
-                    out=w_scales[batch][i:P:32, :, :].bitcast(I32),
+                queue.dma_start(
+                    out=w_scales[batch][i:P:32, :, :].bitcast(word),
                     in_=Wqkv_scales[passes, i:SCALE_ROWS:4, :]
                     .rearrange("g q n -> q g n")
-                    .bitcast(I32),
+                    .bitcast(word),
                 )
-
-        def load_batch(batch):
-            load_w_scales(batch)
-            for r in range(batch * BATCH_ROUNDS, (batch + 1) * BATCH_ROUNDS):
-                load_w_words(r)
-                if r + 2 < ROUNDS:
-                    load_x(r + 2)
 
         load_x(0)
         load_x(1)
-        load_batch(0)
+        load_w_scales(0, nc.vector, nc.sync, I32)
+        for batch in range(1, BATCHES):
+            load_w_scales(batch, nc.gpsimd, nc.gpsimd, F32)
+        for r in range(ROUNDS):
+            load_w_words(r)
+            if r + 2 < ROUNDS:
+                load_x(r + 2)
 
         angle = keep.tile([P, ANGLES], F32, name="angle")
         nc.vector.memset(angle[:, 0:1], SEQ)
@@ -331,8 +330,6 @@ def tile_multiheadattention_pa_k_kernel(
                 sort_words(r + 1)
             if 0 <= r - 2 < V_STREAMED:
                 add_v(r - 2)
-            if r < BATCHES:
-                load_batch(r)
             if r < ROUNDS:
                 transpose_and_regroup(r)
             multiply_qk(r - 1)

@@ -32,7 +32,7 @@ SCALE_ROWS = K_PASS // 32
 BATCH_ROUNDS = 2
 SCALE_BATCH = BATCH_ROUNDS * ROUND
 BATCHES = PASSES // SCALE_BATCH
-V_LAST = 4
+V_LAST = 6
 V_STREAMED = ROUNDS - V_LAST
 
 FLOPS = 2 * TOKENS * K * N_ALL
@@ -129,11 +129,11 @@ def tile_multiheadattention_pa_k_kernel(
                     .bitcast(word),
                 )
 
-        load_x(0)
-        load_x(1)
-        load_w_scales(0, nc.vector, nc.sync, I32)
+        load_w_scales(0, nc.vector, nc.scalar, F32)
         for batch in range(1, BATCHES):
             load_w_scales(batch, nc.gpsimd, nc.gpsimd, F32)
+        load_x(0)
+        load_x(1)
         for r in range(ROUNDS):
             load_w_words(r)
             if r + 2 < ROUNDS:
@@ -337,61 +337,54 @@ def tile_multiheadattention_pa_k_kernel(
                 multiply_v(r - 1, 1)
         multiply_v(V_STREAMED, V_LAST)
 
-        mixed = {}
-        norm = {}
-
-        def mix(tt):
-            t = stream.tile([P, N_QK], F32, name="t")
-            nc.vector.tensor_tensor(out=t[:], in0=acc_qk[tt][:], in1=bias_qk[:], op=ALU.add)
-            t_cos = stream.tile([P, N_QK], F32, name="t_cos")
-            nc.vector.tensor_tensor(out=t_cos[:], in0=t[:], in1=cos_full[:], op=ALU.mult)
-            rot_sin = stream.tile([P, N_QK], F32, name="rot_sin")
-            t_pairs = t[:].rearrange("p (h i e) -> p h i e", h=2, e=2)
-            rot_halves = rot_sin[:].rearrange("p (h f i) -> p h f i", h=2, f=2)
-            sin_by_half = sin_full[:].rearrange("p (h f i) -> p h f i", h=2, f=2)
-            for f in range(2):
+        token_tiles = range(TOKEN_TILES)
+        t = [stream.tile([P, N_QK], F32, name="t") for tt in token_tiles]
+        t_cos = [stream.tile([P, N_QK], F32, name="t_cos") for tt in token_tiles]
+        rot_sin = [stream.tile([P, N_QK], F32, name="rot_sin") for tt in token_tiles]
+        mixed = [stream.tile([P, N_QK], F32, name="mixed") for tt in token_tiles]
+        norm = [stream.tile([P, 2], F32, name="norm") for tt in token_tiles]
+        sin_by_half = sin_full[:].rearrange("p (h f i) -> p h f i", h=2, f=2)
+        for tt in token_tiles:
+            nc.vector.tensor_tensor(out=t[tt][:], in0=acc_qk[tt][:], in1=bias_qk[:], op=ALU.add)
+        for tt in token_tiles:
+            nc.vector.tensor_tensor(out=t_cos[tt][:], in0=t[tt][:], in1=cos_full[:], op=ALU.mult)
+        for f in range(2):
+            for tt in token_tiles:
                 nc.vector.tensor_tensor(
-                    out=rot_halves[:, :, f, :],
-                    in0=t_pairs[:, :, :, 1 - f],
+                    out=rot_sin[tt][:].rearrange("p (h f i) -> p h f i", h=2, f=2)[:, :, f, :],
+                    in0=t[tt][:].rearrange("p (h i e) -> p h i e", h=2, e=2)[:, :, :, 1 - f],
                     in1=sin_by_half[:, :, f, :],
                     op=ALU.mult,
                 )
-            mixed[tt] = stream.tile([P, 2, E], F32, name="mixed")
+        for tt in token_tiles:
             nc.vector.tensor_tensor(
-                out=mixed[tt][:].rearrange("p h e -> p (h e)"),
-                in0=t_cos[:],
-                in1=rot_sin[:],
-                op=ALU.add,
+                out=mixed[tt][:], in0=t_cos[tt][:], in1=rot_sin[tt][:], op=ALU.add
             )
-            squares = stream.tile([P, 2, E], F32, name="squares")
             square_sum = stream.tile([P, 2], F32, name="square_sum")
             for h in range(2):
                 nc.scalar.activation(
-                    out=squares[:, h, :],
-                    in_=mixed[tt][:, h, :],
+                    out=t[tt][:, h * E : (h + 1) * E],
+                    in_=mixed[tt][:, h * E : (h + 1) * E],
                     func=ACT.Square,
                     accum_out=square_sum[:, h : h + 1],
                 )
-            norm[tt] = stream.tile([P, 2], F32, name="norm")
             nc.scalar.sqrt(out=norm[tt][:], in_=square_sum[:])
 
-        def normalise_and_store(tt):
+        for tt in token_tiles:
             inverse = stream.tile([P, 2], F32, name="inverse")
             nc.vector.tensor_scalar_max(out=inverse[:], in0=norm[tt][:], scalar1=NORM_EPS)
             nc.vector.reciprocal(out=inverse[:], in_=inverse[:])
-            unit = stream.tile([P, 2, E], F32, name="unit")
+            unit = t_cos[tt]
             nc.vector.tensor_scalar_mul(
-                out=unit[:, 0, :], in0=mixed[tt][:, 0, :], scalar1=inverse[:, 0:1]
+                out=unit[:, 0:E], in0=mixed[tt][:, 0:E], scalar1=inverse[:, 0:1]
             )
             nc.scalar.activation(
-                out=unit[:, 1, :], in_=mixed[tt][:, 1, :], func=ACT.Copy, scale=inverse[:, 1:2]
+                out=unit[:, E:N_QK], in_=mixed[tt][:, E:N_QK], func=ACT.Copy, scale=inverse[:, 1:2]
             )
             for h in range(2):
-                nc.sync.dma_start(out=qk_rows[h][tt * P : (tt + 1) * P, :], in_=unit[:, h, :])
+                nc.sync.dma_start(
+                    out=qk_rows[h][tt * P : (tt + 1) * P, :], in_=unit[:, h * E : (h + 1) * E]
+                )
 
-        mix(0)
-        mix(1)
-        normalise_and_store(0)
         add_v(V_STREAMED)
         nc.sync.dma_start(out=v_rows.rearrange("(t p) e -> p t e", p=P), in_=v_sum[:])
-        normalise_and_store(1)

@@ -29,11 +29,11 @@ N_V = 128
 V_HALVES = E // N_V
 N_ALL = 3 * E
 SCALE_ROWS = K_PASS // 32
-BATCH_ROUNDS = 2
-SCALE_BATCH = BATCH_ROUNDS * ROUND
-BATCHES = PASSES // SCALE_BATCH
-V_LAST = 6
+URGENT_ROUNDS = 2
+SCALE_BATCH = 2 * ROUND
+V_LAST = 4
 V_STREAMED = ROUNDS - V_LAST
+QK_LAST = 2
 
 FLOPS = 2 * TOKENS * K * N_ALL
 
@@ -71,10 +71,18 @@ def tile_multiheadattention_pa_k_kernel(
             keep.tile([P, ROUND, 2 * N_ALL], U8, name="w_words%d" % r, align_bytes=64)
             for r in range(ROUNDS)
         ]
-        w_scales = [
-            keep.tile([P, SCALE_BATCH, N_ALL], U8, name="w_scales%d" % batch, align_bytes=64)
-            for batch in range(BATCHES)
+        scale_batches = [(r * ROUND, ROUND) for r in range(URGENT_ROUNDS)] + [
+            (first, SCALE_BATCH) for first in range(URGENT_ROUNDS * ROUND, PASSES, SCALE_BATCH)
         ]
+        w_scales = [
+            keep.tile([P, passes, N_ALL], U8, name="w_scales%d" % first, align_bytes=64)
+            for first, passes in scale_batches
+        ]
+        scales_of_pass = {
+            first + j: (tile, j)
+            for (first, passes), tile in zip(scale_batches, w_scales)
+            for j in range(passes)
+        }
         identity = keep.tile([P, P], F32, name="identity")
         ones = keep.tile([P, P], BF16, name="ones")
         bias_row = keep.tile([P, N_ALL], BF16, name="bias_row")
@@ -120,21 +128,22 @@ def tile_multiheadattention_pa_k_kernel(
 
         def load_w_scales(batch, zeroing_engine, queue, word):
             zeroing_engine.memset(w_scales[batch][:].bitcast(word), 0)
-            passes = slice(batch * SCALE_BATCH, (batch + 1) * SCALE_BATCH)
+            first, passes = scale_batches[batch]
             for i in range(4):
                 queue.dma_start(
                     out=w_scales[batch][i:P:32, :, :].bitcast(word),
-                    in_=Wqkv_scales[passes, i:SCALE_ROWS:4, :]
+                    in_=Wqkv_scales[first : first + passes, i:SCALE_ROWS:4, :]
                     .rearrange("g q n -> q g n")
                     .bitcast(word),
                 )
 
-        load_w_scales(0, nc.vector, nc.scalar, F32)
-        for batch in range(1, BATCHES):
+        for batch in range(URGENT_ROUNDS, len(scale_batches)):
             load_w_scales(batch, nc.gpsimd, nc.gpsimd, F32)
         load_x(0)
         load_x(1)
         for r in range(ROUNDS):
+            if r < URGENT_ROUNDS:
+                load_w_scales(r, nc.vector, nc.sync, I32)
             load_w_words(r)
             if r + 2 < ROUNDS:
                 load_x(r + 2)
@@ -262,7 +271,7 @@ def tile_multiheadattention_pa_k_kernel(
                 )
 
         def mx_pass(out, r, tt, g, first_column, columns, start, stop):
-            batch, pass_in_batch = divmod(r * ROUND + g, SCALE_BATCH)
+            scale_tile, pass_in_tile = scales_of_pass[r * ROUND + g]
             nc.tensor.matmul_mx(
                 out=out,
                 lhsT=x_words[r][:, tt, g, :].bitcast(FP8X4),
@@ -270,26 +279,25 @@ def tile_multiheadattention_pa_k_kernel(
                 rhs=w_words[r][:, g, 2 * first_column : 2 * (first_column + columns)].bitcast(
                     FP4X4
                 ),
-                rhs_scale=w_scales[batch][
-                    :, pass_in_batch, first_column : first_column + columns
-                ],
+                rhs_scale=scale_tile[:, pass_in_tile, first_column : first_column + columns],
                 start=start,
                 stop=stop,
             )
 
-        def multiply_qk(r):
+        def multiply_qk(first_round, rounds):
             for tt in range(TOKEN_TILES):
-                for g in range(ROUND):
-                    mx_pass(
-                        acc_qk[tt][:],
-                        r,
-                        tt,
-                        g,
-                        0,
-                        N_QK,
-                        start=(r == 0 and g == 0),
-                        stop=(r == ROUNDS - 1 and g == ROUND - 1),
-                    )
+                for r in range(first_round, first_round + rounds):
+                    for g in range(ROUND):
+                        mx_pass(
+                            acc_qk[tt][:],
+                            r,
+                            tt,
+                            g,
+                            0,
+                            N_QK,
+                            start=(r == 0 and g == 0),
+                            stop=(r == ROUNDS - 1 and g == ROUND - 1),
+                        )
 
         def multiply_v(first_round, rounds):
             v_part[first_round] = psum.tile(
@@ -332,59 +340,68 @@ def tile_multiheadattention_pa_k_kernel(
                 add_v(r - 2)
             if r < ROUNDS:
                 transpose_and_regroup(r)
-            multiply_qk(r - 1)
+            if r - 1 < ROUNDS - QK_LAST:
+                multiply_qk(r - 1, 1)
             if r - 1 < V_STREAMED:
                 multiply_v(r - 1, 1)
+        multiply_qk(ROUNDS - QK_LAST, QK_LAST)
         multiply_v(V_STREAMED, V_LAST)
 
-        token_tiles = range(TOKEN_TILES)
-        t = [stream.tile([P, N_QK], F32, name="t") for tt in token_tiles]
-        t_cos = [stream.tile([P, N_QK], F32, name="t_cos") for tt in token_tiles]
-        rot_sin = [stream.tile([P, N_QK], F32, name="rot_sin") for tt in token_tiles]
-        mixed = [stream.tile([P, N_QK], F32, name="mixed") for tt in token_tiles]
-        norm = [stream.tile([P, 2], F32, name="norm") for tt in token_tiles]
-        sin_by_half = sin_full[:].rearrange("p (h f i) -> p h f i", h=2, f=2)
-        for tt in token_tiles:
-            nc.vector.tensor_tensor(out=t[tt][:], in0=acc_qk[tt][:], in1=bias_qk[:], op=ALU.add)
-        for tt in token_tiles:
-            nc.vector.tensor_tensor(out=t_cos[tt][:], in0=t[tt][:], in1=cos_full[:], op=ALU.mult)
-        for f in range(2):
-            for tt in token_tiles:
+        mixed = {}
+        norm = {}
+
+        def mix(tt):
+            t = stream.tile([P, N_QK], F32, name="t")
+            nc.vector.tensor_tensor(out=t[:], in0=acc_qk[tt][:], in1=bias_qk[:], op=ALU.add)
+            t_cos = stream.tile([P, N_QK], F32, name="t_cos")
+            nc.vector.tensor_tensor(out=t_cos[:], in0=t[:], in1=cos_full[:], op=ALU.mult)
+            rot_sin = stream.tile([P, N_QK], F32, name="rot_sin")
+            t_pairs = t[:].rearrange("p (h i e) -> p h i e", h=2, e=2)
+            rot_halves = rot_sin[:].rearrange("p (h f i) -> p h f i", h=2, f=2)
+            sin_by_half = sin_full[:].rearrange("p (h f i) -> p h f i", h=2, f=2)
+            for f in range(2):
                 nc.vector.tensor_tensor(
-                    out=rot_sin[tt][:].rearrange("p (h f i) -> p h f i", h=2, f=2)[:, :, f, :],
-                    in0=t[tt][:].rearrange("p (h i e) -> p h i e", h=2, e=2)[:, :, :, 1 - f],
+                    out=rot_halves[:, :, f, :],
+                    in0=t_pairs[:, :, :, 1 - f],
                     in1=sin_by_half[:, :, f, :],
                     op=ALU.mult,
                 )
-        for tt in token_tiles:
-            nc.vector.tensor_tensor(
-                out=mixed[tt][:], in0=t_cos[tt][:], in1=rot_sin[tt][:], op=ALU.add
-            )
+            mixed[tt] = stream.tile([P, 2, E], F32, name="mixed")
+            squares = stream.tile([P, 2, E], F32, name="squares")
             square_sum = stream.tile([P, 2], F32, name="square_sum")
             for h in range(2):
+                nc.vector.tensor_tensor(
+                    out=mixed[tt][:, h, :],
+                    in0=t_cos[:, h * E : (h + 1) * E],
+                    in1=rot_sin[:, h * E : (h + 1) * E],
+                    op=ALU.add,
+                )
                 nc.scalar.activation(
-                    out=t[tt][:, h * E : (h + 1) * E],
-                    in_=mixed[tt][:, h * E : (h + 1) * E],
+                    out=squares[:, h, :],
+                    in_=mixed[tt][:, h, :],
                     func=ACT.Square,
                     accum_out=square_sum[:, h : h + 1],
                 )
+            norm[tt] = stream.tile([P, 2], F32, name="norm")
             nc.scalar.sqrt(out=norm[tt][:], in_=square_sum[:])
 
-        for tt in token_tiles:
+        def normalise_and_store(tt):
             inverse = stream.tile([P, 2], F32, name="inverse")
             nc.vector.tensor_scalar_max(out=inverse[:], in0=norm[tt][:], scalar1=NORM_EPS)
             nc.vector.reciprocal(out=inverse[:], in_=inverse[:])
-            unit = t_cos[tt]
+            unit = stream.tile([P, 2, E], F32, name="unit")
             nc.vector.tensor_scalar_mul(
-                out=unit[:, 0:E], in0=mixed[tt][:, 0:E], scalar1=inverse[:, 0:1]
+                out=unit[:, 0, :], in0=mixed[tt][:, 0, :], scalar1=inverse[:, 0:1]
             )
             nc.scalar.activation(
-                out=unit[:, E:N_QK], in_=mixed[tt][:, E:N_QK], func=ACT.Copy, scale=inverse[:, 1:2]
+                out=unit[:, 1, :], in_=mixed[tt][:, 1, :], func=ACT.Copy, scale=inverse[:, 1:2]
             )
             for h in range(2):
-                nc.sync.dma_start(
-                    out=qk_rows[h][tt * P : (tt + 1) * P, :], in_=unit[:, h * E : (h + 1) * E]
-                )
+                nc.sync.dma_start(out=qk_rows[h][tt * P : (tt + 1) * P, :], in_=unit[:, h, :])
 
+        mix(0)
+        mix(1)
+        normalise_and_store(0)
         add_v(V_STREAMED)
         nc.sync.dma_start(out=v_rows.rearrange("(t p) e -> p t e", p=P), in_=v_sum[:])
+        normalise_and_store(1)

@@ -299,16 +299,16 @@ def tile_multiheadattention_pa_k_kernel(
                             stop=(r == ROUNDS - 1 and g == ROUND - 1),
                         )
 
-        def multiply_v(first_round, rounds):
-            v_part[first_round] = psum.tile(
+        def multiply_v(first_round, rounds, token_tiles):
+            v_part[(first_round, token_tiles[0])] = psum.tile(
                 [P, TOKEN_TILES, V_HALVES, N_V], F32, name="v_part", bufs=2
             )
-            for tt in range(TOKEN_TILES):
+            for tt in token_tiles:
                 for half in range(V_HALVES):
                     for r in range(first_round, first_round + rounds):
                         for g in range(ROUND):
                             mx_pass(
-                                v_part[first_round][:, tt, half, :],
+                                v_part[(first_round, token_tiles[0])][:, tt, half, :],
                                 r,
                                 tt,
                                 g,
@@ -321,7 +321,7 @@ def tile_multiheadattention_pa_k_kernel(
         def add_v(first_round):
             nc.vector.tensor_tensor(
                 out=v_sum[:].rearrange("p t e -> p (t e)"),
-                in0=v_part[first_round][:].rearrange("p t h n -> p (t h n)"),
+                in0=v_part[(first_round, 0)][:].rearrange("p t h n -> p (t h n)"),
                 in1=v_sum[:].rearrange("p t e -> p (t e)"),
                 op=ALU.add,
             )
@@ -343,9 +343,10 @@ def tile_multiheadattention_pa_k_kernel(
             if r - 1 < ROUNDS - QK_LAST:
                 multiply_qk(r - 1, 1)
             if r - 1 < V_STREAMED:
-                multiply_v(r - 1, 1)
+                multiply_v(r - 1, 1, [0, 1])
         multiply_qk(ROUNDS - QK_LAST, QK_LAST)
-        multiply_v(V_STREAMED, V_LAST)
+        for tt in range(TOKEN_TILES):
+            multiply_v(V_STREAMED, V_LAST, [tt])
 
         mixed = {}
         norm = {}
@@ -399,9 +400,18 @@ def tile_multiheadattention_pa_k_kernel(
             for h in range(2):
                 nc.sync.dma_start(out=qk_rows[h][tt * P : (tt + 1) * P, :], in_=unit[:, h, :])
 
+        def finish_v(tt):
+            nc.vector.tensor_tensor(
+                out=v_sum[:, tt, :],
+                in0=v_part[(V_STREAMED, tt)][:, tt, :, :].rearrange("p h n -> p (h n)"),
+                in1=v_sum[:, tt, :],
+                op=ALU.add,
+            )
+            nc.sync.dma_start(out=v_rows[tt * P : (tt + 1) * P, :], in_=v_sum[:, tt, :])
+
         mix(0)
         mix(1)
         normalise_and_store(0)
-        add_v(V_STREAMED)
-        nc.sync.dma_start(out=v_rows.rearrange("(t p) e -> p t e", p=P), in_=v_sum[:])
+        finish_v(0)
         normalise_and_store(1)
+        finish_v(1)

import math
from contextlib import ExitStack

import concourse.mybir as mybir
from concourse.masks import make_identity

F32 = mybir.dt.float32
BF16 = mybir.dt.bfloat16
I32 = mybir.dt.int32
U32 = mybir.dt.uint32
U8 = mybir.dt.uint8
FP8X4 = mybir.dt.float8_e4m3fn_x4
FP4X4 = mybir.dt.float4_e2m1fn_x4
ALU = mybir.AluOpType
ACT = mybir.ActivationFunctionType

P = 128
TOKENS = 256
TOKEN_TILES = TOKENS // P
K = 16384
K_PASS = 4 * P
PASSES = K // K_PASS
ROUND = 4
ROUNDS = PASSES // ROUND
PAIR = 2
E = 256
N_QK = 2 * E
N_V = 128
V_HALVES = E // N_V
N_ALL = 3 * E
SCALE_ROWS = K_PASS // 32
URGENT_ROUNDS = 2
SCALE_BATCH = 2 * ROUND
V_LAST = 4
V_STREAMED = ROUNDS - V_LAST
QK_LAST = 2

FLOPS = 2 * TOKENS * K * N_ALL

SEQ = 64.0
ROPE_BASE = 10000.0
ANGLES = E // 2
ANGLE_RATIO = ROPE_BASE ** (-1.0 / ANGLES)
ANGLE_DOUBLINGS = 7
assert 2**ANGLE_DOUBLINGS == ANGLES
NORM_EPS = 1e-12
ROUND_MAGIC = 12582912.0
TWO_PI_HIGH = 6.28125
TWO_PI_LOW = 2.0 * math.pi - TWO_PI_HIGH


def tile_multiheadattention_pa_k_kernel(
    tc, x, Wqkv_words, Wqkv_scales, bqkv, out_0, out_1, out_2
):
    nc = tc.nc
    x_rows = x.flatten_outer_dims()
    qk_rows = [out_0.flatten_outer_dims(), out_1.flatten_outer_dims()]
    v_rows = out_2.flatten_outer_dims()

    with ExitStack() as stack:
        keep = stack.enter_context(tc.tile_pool(name="keep", bufs=1))
        stream = stack.enter_context(tc.tile_pool(name="stream", bufs=2))
        psum = stack.enter_context(tc.psum_pool(name="psum", bufs=1))
        stack.enter_context(tc.manual_schedule())

        x_raw = [
            keep.tile([P, TOKEN_TILES, ROUND * K_PASS], BF16, name="x_raw%d" % r)
            for r in range(ROUNDS)
        ]
        w_words = [
            keep.tile([P, ROUND, 2 * N_ALL], U8, name="w_words%d" % r, align_bytes=64)
            for r in range(ROUNDS)
        ]
        scale_batches = [(r * ROUND, ROUND) for r in range(URGENT_ROUNDS)] + [
            (first, SCALE_BATCH) for first in range(URGENT_ROUNDS * ROUND, PASSES, SCALE_BATCH)
        ]
        w_scales = [
            keep.tile([P, passes, N_ALL], U8, name="w_scales%d" % first, align_bytes=64)
            for first, passes in scale_batches
        ]
        scales_of_pass = {
            first + j: (tile, j)
            for (first, passes), tile in zip(scale_batches, w_scales)
            for j in range(passes)
        }
        identity = keep.tile([P, P], F32, name="identity")
        ones = keep.tile([P, P], BF16, name="ones")
        bias_row = keep.tile([P, N_ALL], BF16, name="bias_row")
        bias_qk = keep.tile([P, N_QK], F32, name="bias_qk")
        v_sum = keep.tile([P, TOKEN_TILES, E], F32, name="v_sum")
        cos_full = keep.tile([P, N_QK], F32, name="cos_full")
        sin_full = keep.tile([P, N_QK], F32, name="sin_full")
        acc_qk = [psum.tile([P, N_QK], F32, name="acc_qk%d" % tt) for tt in range(TOKEN_TILES)]

        make_identity(nc, identity[:])

        nc.vector.memset(bias_row[:], 0.0)
        nc.scalar.dma_start(out=bias_row[0:1, :], in_=bqkv.rearrange("(o n) -> o n", o=1))
        nc.vector.memset(ones[:], 1.0)

        def spread_bias():
            bias_qk_ps = psum.tile([P, N_QK], F32, name="bias_qk_ps", tag="v_part", bufs=2)
            nc.tensor.matmul(
                out=bias_qk_ps[:], lhsT=ones[:], rhs=bias_row[:, 0:N_QK], start=True, stop=True
            )
            bias_v_ps = psum.tile([P, E], F32, name="bias_v_ps", tag="v_part", bufs=2)
            nc.tensor.matmul(
                out=bias_v_ps[:], lhsT=ones[:], rhs=bias_row[:, N_QK:N_ALL], start=True, stop=True
            )
            nc.vector.tensor_copy(out=bias_qk[:], in_=bias_qk_ps[:])
            for tt in range(TOKEN_TILES):
                nc.vector.tensor_copy(out=v_sum[:, tt, :], in_=bias_v_ps[:])

        def load_x(r):
            columns = slice(r * ROUND * K_PASS, (r + 1) * ROUND * K_PASS)
            for tt in range(TOKEN_TILES):
                nc.sync.dma_start(
                    out=x_raw[r][:, tt, :], in_=x_rows[tt * P : (tt + 1) * P, columns]
                )

        def load_w_words(r):
            nc.sync.dma_start(
                out=w_words[r][:].bitcast(I32),
                in_=Wqkv_words[r * ROUND : (r + 1) * ROUND]
                .rearrange("g p b -> p g b")
                .bitcast(I32),
            )

        def load_w_scales(batch, zeroing_engine, queue, word):
            zeroing_engine.memset(w_scales[batch][:].bitcast(word), 0)
            first, passes = scale_batches[batch]
            for i in range(4):
                queue.dma_start(
                    out=w_scales[batch][i:P:32, :, :].bitcast(word),
                    in_=Wqkv_scales[first : first + passes, i:SCALE_ROWS:4, :]
                    .rearrange("g q n -> q g n")
                    .bitcast(word),
                )

        for batch in range(URGENT_ROUNDS, len(scale_batches)):
            load_w_scales(batch, nc.gpsimd, nc.gpsimd, F32)
        load_x(0)
        load_x(1)
        for r in range(ROUNDS):
            if r < URGENT_ROUNDS:
                load_w_scales(r, nc.vector, nc.sync, I32)
            load_w_words(r)
            if r + 2 < ROUNDS:
                load_x(r + 2)

        angle = keep.tile([P, ANGLES], F32, name="angle")
        nc.vector.memset(angle[:, 0:1], SEQ)
        for doubling in range(ANGLE_DOUBLINGS):
            span = 2**doubling
            nc.vector.tensor_scalar_mul(
                out=angle[:, span : 2 * span], in0=angle[:, 0:span], scalar1=ANGLE_RATIO**span
            )
        turns = keep.tile([P, ANGLES], F32, name="turns")
        nc.vector.tensor_scalar(
            out=turns[:],
            in0=angle[:],
            scalar1=1.0 / (2.0 * math.pi),
            scalar2=ROUND_MAGIC,
            op0=ALU.mult,
            op1=ALU.add,
        )
        nc.vector.tensor_scalar_sub(out=turns[:], in0=turns[:], scalar1=ROUND_MAGIC)
        reduced = keep.tile([P, ANGLES], F32, name="reduced")
        nc.vector.scalar_tensor_tensor(
            out=reduced[:],
            in0=turns[:],
            scalar=-TWO_PI_HIGH,
            in1=angle[:],
            op0=ALU.mult,
            op1=ALU.add,
        )
        nc.vector.scalar_tensor_tensor(
            out=reduced[:],
            in0=turns[:],
            scalar=-TWO_PI_LOW,
            in1=reduced[:],
            op0=ALU.mult,
            op1=ALU.add,
        )
        quarter_minus_abs = keep.tile([P, ANGLES], F32, name="quarter_minus_abs")
        nc.vector.scalar_tensor_tensor(
            out=quarter_minus_abs[:],
            in0=reduced[:],
            scalar=-1.0,
            in1=reduced[:],
            op0=ALU.mult,
            op1=ALU.max,
        )
        nc.vector.tensor_scalar(
            out=quarter_minus_abs[:],
            in0=quarter_minus_abs[:],
            scalar1=-1.0,
            scalar2=math.pi / 2.0,
            op0=ALU.mult,
            op1=ALU.add,
        )
        nc.scalar.activation(
            out=cos_full[:].rearrange("p (h j e) -> p h j e", h=2, e=2),
            in_=quarter_minus_abs[:].unsqueeze(1).unsqueeze(3).to_broadcast([P, 2, ANGLES, 2]),
            func=ACT.Sin,
        )
        sin_halves = sin_full[:].rearrange("p (h f j e) -> p h f j e", h=2, f=2, e=2)
        for f in range(2):
            nc.scalar.activation(
                out=sin_halves[:, :, f, :, :],
                in_=reduced[:, f * (ANGLES // 2) : (f + 1) * (ANGLES // 2)]
                .unsqueeze(1)
                .unsqueeze(3)
                .to_broadcast([P, 2, ANGLES // 2, 2]),
                func=ACT.Sin,
                scale=(-1.0 if f == 0 else 1.0),
            )
        sorted_x = {}
        grouped = {}
        x_words = {}
        x_scales = {}
        v_part = {}

        def sort_words(r):
            sorted_x[r] = stream.tile([P, TOKEN_TILES, ROUND, 2, P], F32, name="sorted_x")
            for tt in range(TOKEN_TILES):
                nc.vector.tensor_copy(
                    out=sorted_x[r][:, tt, :, :, :],
                    in_=x_raw[r][:, tt, :]
                    .bitcast(F32)
                    .rearrange("p (g w u) -> p g u w", g=ROUND, u=2),
                )

        def transpose_and_regroup(r):
            grouped[r] = stream.tile(
                [P, TOKEN_TILES, ROUND, 4 * P], BF16, name="grouped", align_bytes=64
            )
            banks = {}
            for tt in range(TOKEN_TILES):
                for pair in range(ROUND // PAIR):
                    bank = psum.tile([P, PAIR, 2, P], F32, name="bank", tag="transposed", bufs=4)
                    banks[(tt, pair)] = bank
                    for a in range(PAIR):
                        for u in range(2):
                            nc.tensor.transpose(
                                out=bank[:, a, u, :],
                                in_=sorted_x[r][:, tt, pair * PAIR + a, u, :],
                                identity=identity[:],
                            )
            for tt in range(TOKEN_TILES):
                for pair in range(ROUND // PAIR):
                    nc.scalar.copy(
                        out=grouped[r][:, tt, pair * PAIR : (pair + 1) * PAIR, :]
                        .bitcast(F32)
                        .rearrange("p a (t u) -> p a t u", u=2),
                        in_=banks[(tt, pair)][:].rearrange("p a u t -> p a t u"),
                    )

        def quantise(r):
            x_words[r] = stream.tile(
                [P, TOKEN_TILES, ROUND, P], U32, name="x_words", bufs=V_LAST, align_bytes=64
            )
            x_scales[r] = stream.tile(
                [P, TOKEN_TILES, ROUND, P], U8, name="x_scales", bufs=V_LAST, align_bytes=64
            )
            for tt in range(TOKEN_TILES):
                nc.vector.quantize_mx(
                    out=x_words[r][:, tt, :, :].rearrange("p g t -> p (g t)").bitcast(FP8X4),
                    scales=x_scales[r][:, tt, :, :].rearrange("p g t -> p (g t)"),
                    in_=grouped[r][:, tt, :, :].rearrange("p g c -> p (g c)"),
                )

        def mx_pass(out, r, tt, g, first_column, columns, start, stop):
            scale_tile, pass_in_tile = scales_of_pass[r * ROUND + g]
            nc.tensor.matmul_mx(
                out=out,
                lhsT=x_words[r][:, tt, g, :].bitcast(FP8X4),
                lhsT_scale=x_scales[r][:, tt, g, :],
                rhs=w_words[r][:, g, 2 * first_column : 2 * (first_column + columns)].bitcast(
                    FP4X4
                ),
                rhs_scale=scale_tile[:, pass_in_tile, first_column : first_column + columns],
                start=start,
                stop=stop,
            )

        def multiply_qk(first_round, rounds):
            for tt in range(TOKEN_TILES):
                for r in range(first_round, first_round + rounds):
                    for g in range(ROUND):
                        mx_pass(
                            acc_qk[tt][:],
                            r,
                            tt,
                            g,
                            0,
                            N_QK,
                            start=(r == 0 and g == 0),
                            stop=(r == ROUNDS - 1 and g == ROUND - 1),
                        )

        def multiply_v(first_round, rounds, token_tiles):
            v_part[(first_round, token_tiles[0])] = psum.tile(
                [P, TOKEN_TILES, V_HALVES, N_V], F32, name="v_part", bufs=2
            )
            for tt in token_tiles:
                for half in range(V_HALVES):
                    for r in range(first_round, first_round + rounds):
                        for g in range(ROUND):
                            mx_pass(
                                v_part[(first_round, token_tiles[0])][:, tt, half, :],
                                r,
                                tt,
                                g,
                                N_QK + half * N_V,
                                N_V,
                                start=(r == first_round and g == 0),
                                stop=(r == first_round + rounds - 1 and g == ROUND - 1),
                            )

        def add_v(first_round):
            nc.vector.tensor_tensor(
                out=v_sum[:].rearrange("p t e -> p (t e)"),
                in0=v_part[(first_round, 0)][:].rearrange("p t h n -> p (t h n)"),
                in1=v_sum[:].rearrange("p t e -> p (t e)"),
                op=ALU.add,
            )

        sort_words(0)
        transpose_and_regroup(0)
        sqrt_warm = keep.tile([P, 1], F32, name="sqrt_warm")
        nc.scalar.sqrt(out=sqrt_warm[:], in_=angle[:, 0:1])
        sort_words(1)
        spread_bias()
        for r in range(1, ROUNDS + 1):
            quantise(r - 1)
            if r + 1 < ROUNDS:
                sort_words(r + 1)
            if 0 <= r - 2 < V_STREAMED:
                add_v(r - 2)
            if r < ROUNDS:
                transpose_and_regroup(r)
            if r - 1 < ROUNDS - QK_LAST:
                multiply_qk(r - 1, 1)
            if r - 1 < V_STREAMED:
                multiply_v(r - 1, 1, [0, 1])
        multiply_qk(ROUNDS - QK_LAST, QK_LAST)
        for tt in range(TOKEN_TILES):
            multiply_v(V_STREAMED, V_LAST, [tt])

        mixed = {}
        norm = {}

        def mix(tt):
            t = stream.tile([P, N_QK], F32, name="t")
            nc.vector.tensor_tensor(out=t[:], in0=acc_qk[tt][:], in1=bias_qk[:], op=ALU.add)
            t_cos = stream.tile([P, N_QK], F32, name="t_cos")
            nc.vector.tensor_tensor(out=t_cos[:], in0=t[:], in1=cos_full[:], op=ALU.mult)
            rot_sin = stream.tile([P, N_QK], F32, name="rot_sin")
            t_pairs = t[:].rearrange("p (h i e) -> p h i e", h=2, e=2)
            rot_halves = rot_sin[:].rearrange("p (h f i) -> p h f i", h=2, f=2)
            sin_by_half = sin_full[:].rearrange("p (h f i) -> p h f i", h=2, f=2)
            for f in range(2):
                nc.vector.tensor_tensor(
                    out=rot_halves[:, :, f, :],
                    in0=t_pairs[:, :, :, 1 - f],
                    in1=sin_by_half[:, :, f, :],
                    op=ALU.mult,
                )
            mixed[tt] = stream.tile([P, 2, E], F32, name="mixed")
            squares = stream.tile([P, 2, E], F32, name="squares")
            square_sum = stream.tile([P, 2], F32, name="square_sum")
            for h in range(2):
                nc.vector.tensor_tensor(
                    out=mixed[tt][:, h, :],
                    in0=t_cos[:, h * E : (h + 1) * E],
                    in1=rot_sin[:, h * E : (h + 1) * E],
                    op=ALU.add,
                )
                nc.scalar.activation(
                    out=squares[:, h, :],
                    in_=mixed[tt][:, h, :],
                    func=ACT.Square,
                    accum_out=square_sum[:, h : h + 1],
                )
            norm[tt] = stream.tile([P, 2], F32, name="norm")
            nc.scalar.sqrt(out=norm[tt][:], in_=square_sum[:])

        def normalise_and_store(tt):
            inverse = stream.tile([P, 2], F32, name="inverse")
            nc.vector.tensor_scalar_max(out=inverse[:], in0=norm[tt][:], scalar1=NORM_EPS)
            nc.vector.reciprocal(out=inverse[:], in_=inverse[:])
            unit = stream.tile([P, 2, E], F32, name="unit")
            nc.vector.tensor_scalar_mul(
                out=unit[:, 0, :], in0=mixed[tt][:, 0, :], scalar1=inverse[:, 0:1]
            )
            nc.scalar.activation(
                out=unit[:, 1, :], in_=mixed[tt][:, 1, :], func=ACT.Copy, scale=inverse[:, 1:2]
            )
            for h in range(2):
                nc.sync.dma_start(out=qk_rows[h][tt * P : (tt + 1) * P, :], in_=unit[:, h, :])

        def finish_v(tt):
            nc.vector.tensor_tensor(
                out=v_sum[:, tt, :],
                in0=v_part[(V_STREAMED, tt)][:, tt, :, :].rearrange("p h n -> p (h n)"),
                in1=v_sum[:, tt, :],
                op=ALU.add,
            )
            nc.sync.dma_start(out=v_rows[tt * P : (tt + 1) * P, :], in_=v_sum[:, tt, :])

        mix(0)
        mix(1)
        normalise_and_store(0)
        finish_v(0)
        normalise_and_store(1)
        finish_v(1)
